import numpy as np
import ml_dtypes


def mxq(x, axis, fmt="e4m3"):
    dtype, down = {"e4m3": (ml_dtypes.float8_e4m3fn, 7), "e5m2": (ml_dtypes.float8_e5m2, 14)}[fmt]
    v = np.moveaxis(np.asarray(x, np.float32).astype(ml_dtypes.bfloat16).astype(np.float64), axis, -1)
    blocks = v.reshape(v.shape[:-1] + (-1, 32))
    amax = np.abs(blocks).max(-1, keepdims=True)
    byte = np.maximum(np.where(amax > 0, np.frexp(amax)[1] - 1 + 127, 0) - down, 1)
    scale = np.exp2(byte - 127.0)
    codes = (blocks / scale).astype(np.float32).astype(dtype).astype(np.float64)
    return np.moveaxis((codes * scale).reshape(v.shape), -1, axis)


WIDE = False


def mx_kscale(k):
    if not WIDE:
        return np.ones(k)
    levels = np.array([10, -10, 5, -5, 0])
    a = np.random.permutation(np.resize(levels, k // 512 * 4)).reshape(k // 512, 4)
    idx = np.arange(k)
    return np.exp2(a[idx // 512, idx % 128 // 32])


BF16 = ml_dtypes.bfloat16


def bf(x):
    return np.asarray(x, np.float32).astype(BF16)


def f64(x):
    return np.asarray(x).astype(np.float64)


B, C, L = 2, 512, 2048
BETA_MIN = 1e-06
PEDESTAL = (2.0 ** -18) ** 2


def nn_reparam(p, minimum):
    bound = (minimum + PEDESTAL) ** 0.5
    return np.maximum(p, bound) ** 2 - PEDESTAL


def setup_inputs():
    t = np.exp2(np.round(np.log2(mx_kscale(C)) / 2))
    amp = np.exp2(np.random.uniform(-1.0, 1.0, (B, 1, L)))
    return {"x": bf(np.random.standard_normal((B, C, L)) * amp * t[None, :, None]),
            "beta_param": bf(np.random.standard_normal(C) * t),
            "gamma_param": bf(np.random.standard_normal((C, C)) * np.sqrt(2.0 / C) * t[:, None] / t[None, :])}


def reference(x, beta_param, gamma_param):
    x = f64(x)
    beta = nn_reparam(f64(beta_param), BETA_MIN)
    gamma = nn_reparam(f64(gamma_param), 0.0)
    norm = (mxq(gamma, 1, "e4m3") @ mxq(x * x, 1, "e4m3")) + beta[None, :, None]
    return x * (1.0 / np.sqrt(norm))

@@ -1,0 +1,176 @@
+from contextlib import ExitStack
+
+import concourse.mybir as mybir
+from concourse.masks import make_identity
+
+F32 = mybir.dt.float32
+BF16 = mybir.dt.bfloat16
+U32 = mybir.dt.uint32
+U8 = mybir.dt.uint8
+FP8X4 = mybir.dt.float8_e4m3fn_x4
+ACT = mybir.ActivationFunctionType
+ALU = mybir.AluOpType
+
+B, C, L = 2, 512, 2048
+P = 128
+PACK = 4
+W = 512
+NB = B * L // W
+FLOPS = 2 * B * C * C * L
+PEDESTAL = 2.0 ** -36
+GAMMA_BOUND = 2.0 ** -18
+BETA_BOUND = (1e-6 + PEDESTAL) ** 0.5
+CA = 304
+LOADS = ((0, 0, 512), (0, 512, 512), (0, 1024, 1024), (1, 0, 1024), (1, 1024, 1024))
+
+
+def tile_gdn_1d_kernel(tc, x, beta_param, gamma_param, out):
+    nc = tc.nc
+    with ExitStack() as ctx:
+        const = ctx.enter_context(tc.tile_pool(name="const", bufs=1))
+        grp_pool = ctx.enter_context(tc.tile_pool(name="grp", bufs=3))
+        mx_pool = ctx.enter_context(tc.tile_pool(name="mx", bufs=3))
+        r_pool = ctx.enter_context(tc.tile_pool(name="r", bufs=4))
+        psum = ctx.enter_context(tc.psum_pool(name="psum", bufs=8))
+
+        bp = const.tile([P, PACK], BF16)
+        nc.scalar.dma_start(out=bp[:], in_=beta_param.rearrange("(p j) -> p j", j=PACK))
+        x_tiles = []
+        g_sb = const.tile([P, PACK, C], BF16)
+        for i, (b, l0, width) in enumerate(LOADS):
+            xt = const.tile([P, PACK, width], BF16, name="x%d" % i)
+            nc.sync.dma_start(
+                out=xt[:],
+                in_=x[b].rearrange("(p j) l -> p j l", j=PACK)[:, :, l0 : l0 + width],
+            )
+            x_tiles.append(xt)
+            if i == 0:
+                nc.sync.dma_start(
+                    out=g_sb[:], in_=gamma_param.rearrange("(m j) i -> m j i", j=PACK)
+                )
+
+        def x_block(n):
+            b, l0 = n // (L // W), (n % (L // W)) * W
+            for i, (lb, ll0, width) in enumerate(LOADS):
+                if lb == b and ll0 <= l0 < ll0 + width:
+                    return x_tiles[i][:, :, l0 - ll0 : l0 - ll0 + W]
+            raise ValueError("no load holds block %d" % n)
+
+        ident = const.tile([P, P], F32)
+        make_identity(nc, ident[:])
+        one = const.tile([P, 1], F32)
+        nc.vector.memset(one[:], 1.0)
+        warm = const.tile([P, 1], F32)
+        nc.scalar.activation(out=warm[:], in_=one[:], func=ACT.Abs_reciprocal_sqrt)
+
+        bh = const.tile([P, PACK], F32)
+        nc.vector.tensor_scalar_max(out=bh[:], in0=bp[:], scalar1=BETA_BOUND)
+        bsq = const.tile([P, PACK], F32)
+        nc.vector.tensor_tensor(out=bsq[:], in0=bh[:], in1=bh[:], op=ALU.mult)
+        beta = const.tile([P, PACK], F32)
+        nc.vector.tensor_scalar(
+            out=beta[:], in0=bsq[:], scalar1=PEDESTAL, scalar2=None, op0=ALU.subtract
+        )
+
+        g_codes = const.tile([P, PACK, P], U32, align_bytes=64)
+        g_scales = const.tile([P, PACK, P], U8, align_bytes=64)
+
+        def gamma_prep():
+            h_sb = const.tile([P, PACK, C], BF16)
+            nc.vector.tensor_scalar_max(out=h_sb[:], in0=g_sb[:], scalar1=GAMMA_BOUND)
+            hw = h_sb[:].bitcast(F32).rearrange("m j (p u) -> m j u p", u=2)
+            sq = const.tile([P, PACK, C], F32)
+            gam = const.tile([P, PACK, C], BF16, align_bytes=64)
+            for j in range(PACK):
+                gt = psum.tile([P, 2, P], F32, tag="bank")
+                for u in range(2):
+                    nc.tensor.transpose(gt[:, u, :], hw[:, j, u, :], ident[:])
+                nc.scalar.activation(
+                    out=sq[:, j, :].rearrange("p (m u e) -> p m u e", u=2, e=2),
+                    in_=gt[:].bitcast(BF16).rearrange("p u (m e) -> p m u e", e=2),
+                    func=ACT.Square,
+                )
+                nc.vector.tensor_scalar(
+                    out=gam[:, j, :], in0=sq[:, j, :], scalar1=PEDESTAL, scalar2=None,
+                    op0=ALU.subtract,
+                )
+            for j in range(PACK):
+                nc.vector.quantize_mx(
+                    out=g_codes[:, j, :].bitcast(FP8X4),
+                    scales=g_scales[:, j, :],
+                    in_=gam[:, j, :],
+                )
+
+        grps = {}
+        mxs = {}
+        banks = {}
+
+        def squares(n):
+            xs = x_block(n)
+            grp = grp_pool.tile([P, W, PACK], BF16, align_bytes=64)
+            grps[n] = grp
+            nc.scalar.activation(
+                out=grp[:, 0:CA, :].rearrange("p (c i) t -> p c t i", i=4),
+                in_=xs[:, :, 0:CA].rearrange("p t (c i) -> p c t i", i=4),
+                func=ACT.Square,
+            )
+            src = xs[:, :, CA:W].rearrange("p t (c i) -> p c t i", i=4)
+            nc.vector.tensor_tensor(
+                out=grp[:, CA:W, :].rearrange("p (c i) t -> p c t i", i=4),
+                in0=src, in1=src, op=ALU.mult,
+            )
+
+        def quantise(n):
+            codes = mx_pool.tile([P, W], U32, align_bytes=64)
+            scales = mx_pool.tile([P, W], U8, align_bytes=64)
+            mxs[n] = (codes, scales)
+            nc.vector.quantize_mx(
+                out=codes[:].bitcast(FP8X4),
+                scales=scales[:],
+                in_=grps[n][:].rearrange("p w t -> p (w t)"),
+            )
+
+        def matmuls(n):
+            codes, scales = mxs[n]
+            for j in range(PACK):
+                ps = psum.tile([P, W], F32, tag="bank")
+                banks[(n, j)] = ps
+                nc.tensor.matmul_mx(
+                    out=ps[:],
+                    lhsT=g_codes[:, j, :].bitcast(FP8X4),
+                    lhsT_scale=g_scales[:, j, :],
+                    rhs=codes[:].bitcast(FP8X4),
+                    rhs_scale=scales[:],
+                    start=True,
+                    stop=True,
+                )
+
+        def epilogue(n):
+            xs = x_block(n)
+            b, l0 = n // (L // W), (n % (L // W)) * W
+            r = r_pool.tile([P, PACK, W], F32)
+            for j in range(PACK):
+                nc.scalar.activation(
+                    out=r[:, j, :], in_=banks[(n, j)][:], func=ACT.Abs_reciprocal_sqrt,
+                    bias=beta[:, j : j + 1], scale=1.0,
+                )
+                if j % 2 == 1:
+                    nc.vector.tensor_tensor(
+                        out=r[:, j - 1 : j + 1, :], in0=r[:, j - 1 : j + 1, :],
+                        in1=xs[:, j - 1 : j + 1, :], op=ALU.mult,
+                    )
+            nc.sync.dma_start(
+                out=out[b].rearrange("(p j) l -> p j l", j=PACK)[:, :, l0 : l0 + W],
+                in_=r[:],
+            )
+
+        for s in range(NB + 2):
+            if s < NB:
+                squares(s)
+            if s == 0:
+                gamma_prep()
+            if 1 <= s <= NB:
+                quantise(s - 1)
+                matmuls(s - 1)
+            if s >= 2:
+                epilogue(s - 2)

@@ -20,8 +20,11 @@ FLOPS = 2 * B * C * C * L
 PEDESTAL = 2.0 ** -36
 GAMMA_BOUND = 2.0 ** -18
 BETA_BOUND = (1e-6 + PEDESTAL) ** 0.5
-CA = 304
+MANUAL = True
+CA = (352, 96, 256, 304, 304, 304, 304, 304)
+SG = (2, 2, 2, 2, 2, 2, 2, 1)
 LOADS = ((0, 0, 512), (0, 512, 512), (0, 1024, 1024), (1, 0, 1024), (1, 1024, 1024))
+GAMMA_AFTER = 0
 
 
 def tile_gdn_1d_kernel(tc, x, beta_param, gamma_param, out):
@@ -32,6 +35,8 @@ def tile_gdn_1d_kernel(tc, x, beta_param, gamma_param, out):
         mx_pool = ctx.enter_context(tc.tile_pool(name="mx", bufs=3))
         r_pool = ctx.enter_context(tc.tile_pool(name="r", bufs=4))
         psum = ctx.enter_context(tc.psum_pool(name="psum", bufs=8))
+        if MANUAL:
+            ctx.enter_context(tc.manual_schedule())
 
         bp = const.tile([P, PACK], BF16)
         nc.scalar.dma_start(out=bp[:], in_=beta_param.rearrange("(p j) -> p j", j=PACK))
@@ -44,7 +49,7 @@ def tile_gdn_1d_kernel(tc, x, beta_param, gamma_param, out):
                 in_=x[b].rearrange("(p j) l -> p j l", j=PACK)[:, :, l0 : l0 + width],
             )
             x_tiles.append(xt)
-            if i == 0:
+            if i == GAMMA_AFTER:
                 nc.sync.dma_start(
                     out=g_sb[:], in_=gamma_param.rearrange("(m j) i -> m j i", j=PACK)
                 )
@@ -74,51 +79,67 @@ def tile_gdn_1d_kernel(tc, x, beta_param, gamma_param, out):
 
         g_codes = const.tile([P, PACK, P], U32, align_bytes=64)
         g_scales = const.tile([P, PACK, P], U8, align_bytes=64)
+        h_sb = const.tile([P, PACK, C], BF16)
+        sq = const.tile([P, PACK, C], F32)
+        gam = const.tile([P, PACK, C], BF16, align_bytes=64)
+        gts = {}
 
-        def gamma_prep():
-            h_sb = const.tile([P, PACK, C], BF16)
+        def gamma_floor():
             nc.vector.tensor_scalar_max(out=h_sb[:], in0=g_sb[:], scalar1=GAMMA_BOUND)
+
+        def gamma_transposes():
             hw = h_sb[:].bitcast(F32).rearrange("m j (p u) -> m j u p", u=2)
-            sq = const.tile([P, PACK, C], F32)
-            gam = const.tile([P, PACK, C], BF16, align_bytes=64)
             for j in range(PACK):
                 gt = psum.tile([P, 2, P], F32, tag="bank")
+                gts[j] = gt
                 for u in range(2):
                     nc.tensor.transpose(gt[:, u, :], hw[:, j, u, :], ident[:])
-                nc.scalar.activation(
-                    out=sq[:, j, :].rearrange("p (m u e) -> p m u e", u=2, e=2),
-                    in_=gt[:].bitcast(BF16).rearrange("p u (m e) -> p m u e", e=2),
-                    func=ACT.Square,
-                )
-                nc.vector.tensor_scalar(
-                    out=gam[:, j, :], in0=sq[:, j, :], scalar1=PEDESTAL, scalar2=None,
-                    op0=ALU.subtract,
-                )
-            for j in range(PACK):
-                nc.vector.quantize_mx(
-                    out=g_codes[:, j, :].bitcast(FP8X4),
-                    scales=g_scales[:, j, :],
-                    in_=gam[:, j, :],
-                )
+
+        def gamma_square(j):
+            nc.scalar.activation(
+                out=sq[:, j, :].rearrange("p (m u e) -> p m u e", u=2, e=2),
+                in_=gts[j][:].bitcast(BF16).rearrange("p u (m e) -> p m u e", e=2),
+                func=ACT.Square,
+            )
+
+        def gamma_round(j):
+            nc.vector.tensor_scalar(
+                out=gam[:, j, :], in0=sq[:, j, :], scalar1=PEDESTAL, scalar2=None,
+                op0=ALU.subtract,
+            )
+
+        def gamma_quantise(j):
+            nc.vector.quantize_mx(
+                out=g_codes[:, j, :].bitcast(FP8X4),
+                scales=g_scales[:, j, :],
+                in_=gam[:, j, :],
+            )
 
         grps = {}
         mxs = {}
         banks = {}
 
-        def squares(n):
-            xs = x_block(n)
-            grp = grp_pool.tile([P, W, PACK], BF16, align_bytes=64)
-            grps[n] = grp
-            nc.scalar.activation(
-                out=grp[:, 0:CA, :].rearrange("p (c i) t -> p c t i", i=4),
-                in_=xs[:, :, 0:CA].rearrange("p t (c i) -> p c t i", i=4),
-                func=ACT.Square,
-            )
-            src = xs[:, :, CA:W].rearrange("p t (c i) -> p c t i", i=4)
-            nc.vector.tensor_tensor(
-                out=grp[:, CA:W, :].rearrange("p (c i) t -> p c t i", i=4),
-                in0=src, in1=src, op=ALU.mult,
-            )
+        def grp_tile(n):
+            if n not in grps:
+                grp = grp_pool.tile([P, W, PACK], BF16, align_bytes=64)
+                grps[n] = grp
+            return grps[n]
+
+        def squares_act(n):
+            if CA[n] > 0:
+                nc.scalar.activation(
+                    out=grp_tile(n)[:, 0 : CA[n], :].rearrange("p (c i) t -> p c t i", i=4),
+                    in_=x_block(n)[:, :, 0 : CA[n]].rearrange("p t (c i) -> p c t i", i=4),
+                    func=ACT.Square,
+                )
+
+        def squares_dve(n):
+            if CA[n] < W:
+                src = x_block(n)[:, :, CA[n] : W].rearrange("p t (c i) -> p c t i", i=4)
+                nc.vector.tensor_tensor(
+                    out=grp_tile(n)[:, CA[n] : W, :].rearrange("p (c i) t -> p c t i", i=4),
+                    in0=src, in1=src, op=ALU.mult,
+                )
 
         def quantise(n):
             codes = mx_pool.tile([P, W], U32, align_bytes=64)
@@ -148,29 +169,49 @@ def tile_gdn_1d_kernel(tc, x, beta_param, gamma_param, out):
         def epilogue(n):
             xs = x_block(n)
             b, l0 = n // (L // W), (n % (L // W)) * W
+            out_v = out[b].rearrange("(p j) l -> p j l", j=PACK)[:, :, l0 : l0 + W]
             r = r_pool.tile([P, PACK, W], F32)
+            sg = SG[n]
+            mg = min(sg, 2)
             for j in range(PACK):
                 nc.scalar.activation(
                     out=r[:, j, :], in_=banks[(n, j)][:], func=ACT.Abs_reciprocal_sqrt,
                     bias=beta[:, j : j + 1], scale=1.0,
                 )
-                if j % 2 == 1:
+                if (j + 1) % mg == 0:
+                    js = slice(j + 1 - mg, j + 1)
                     nc.vector.tensor_tensor(
-                        out=r[:, j - 1 : j + 1, :], in0=r[:, j - 1 : j + 1, :],
-                        in1=xs[:, j - 1 : j + 1, :], op=ALU.mult,
+                        out=r[:, js, :], in0=r[:, js, :], in1=xs[:, js, :], op=ALU.mult
                     )
-            nc.sync.dma_start(
-                out=out[b].rearrange("(p j) l -> p j l", j=PACK)[:, :, l0 : l0 + W],
-                in_=r[:],
-            )
+                if (j + 1) % sg == 0:
+                    js = slice(j + 1 - sg, j + 1)
+                    nc.sync.dma_start(out=out_v[:, js, :], in_=r[:, js, :])
 
-        for s in range(NB + 2):
+        squares_act(0)
+        squares_dve(0)
+        gamma_floor()
+        gamma_transposes()
+        quantise(0)
+        squares_dve(1)
+        gamma_square(0)
+        gamma_square(1)
+        gamma_round(0)
+        gamma_round(1)
+        gamma_quantise(0)
+        gamma_square(2)
+        gamma_round(2)
+        gamma_quantise(1)
+        gamma_square(3)
+        gamma_round(3)
+        gamma_quantise(2)
+        gamma_quantise(3)
+        squares_act(1)
+        matmuls(0)
+        for s in range(2, NB + 2):
             if s < NB:
-                squares(s)
-            if s == 0:
-                gamma_prep()
-            if 1 <= s <= NB:
+                squares_act(s)
+                squares_dve(s)
+            if s <= NB:
                 quantise(s - 1)
                 matmuls(s - 1)
-            if s >= 2:
-                epilogue(s - 2)
+            epilogue(s - 2)

@@ -20,9 +20,8 @@ FLOPS = 2 * B * C * C * L
 PEDESTAL = 2.0 ** -36
 GAMMA_BOUND = 2.0 ** -18
 BETA_BOUND = (1e-6 + PEDESTAL) ** 0.5
-MANUAL = True
-CA = (352, 96, 256, 304, 304, 304, 304, 304)
-SG = (2, 2, 2, 2, 2, 2, 2, 1)
+CA = (352, 96, 256, 328, 328, 328, 328, 328)
+SG = (2, 2, 2, 2, 2, 2, 1, 1)
 LOADS = ((0, 0, 512), (0, 512, 512), (0, 1024, 1024), (1, 0, 1024), (1, 1024, 1024))
 GAMMA_AFTER = 0
 
@@ -35,8 +34,7 @@ def tile_gdn_1d_kernel(tc, x, beta_param, gamma_param, out):
         mx_pool = ctx.enter_context(tc.tile_pool(name="mx", bufs=3))
         r_pool = ctx.enter_context(tc.tile_pool(name="r", bufs=4))
         psum = ctx.enter_context(tc.psum_pool(name="psum", bufs=8))
-        if MANUAL:
-            ctx.enter_context(tc.manual_schedule())
+        ctx.enter_context(tc.manual_schedule())
 
         bp = const.tile([P, PACK], BF16)
         nc.scalar.dma_start(out=bp[:], in_=beta_param.rearrange("(p j) -> p j", j=PACK))
@@ -126,20 +124,18 @@ def tile_gdn_1d_kernel(tc, x, beta_param, gamma_param, out):
             return grps[n]
 
         def squares_act(n):
-            if CA[n] > 0:
-                nc.scalar.activation(
-                    out=grp_tile(n)[:, 0 : CA[n], :].rearrange("p (c i) t -> p c t i", i=4),
-                    in_=x_block(n)[:, :, 0 : CA[n]].rearrange("p t (c i) -> p c t i", i=4),
-                    func=ACT.Square,
-                )
+            nc.scalar.activation(
+                out=grp_tile(n)[:, 0 : CA[n], :].rearrange("p (c i) t -> p c t i", i=4),
+                in_=x_block(n)[:, :, 0 : CA[n]].rearrange("p t (c i) -> p c t i", i=4),
+                func=ACT.Square,
+            )
 
         def squares_dve(n):
-            if CA[n] < W:
-                src = x_block(n)[:, :, CA[n] : W].rearrange("p t (c i) -> p c t i", i=4)
-                nc.vector.tensor_tensor(
-                    out=grp_tile(n)[:, CA[n] : W, :].rearrange("p (c i) t -> p c t i", i=4),
-                    in0=src, in1=src, op=ALU.mult,
-                )
+            src = x_block(n)[:, :, CA[n] : W].rearrange("p t (c i) -> p c t i", i=4)
+            nc.vector.tensor_tensor(
+                out=grp_tile(n)[:, CA[n] : W, :].rearrange("p (c i) t -> p c t i", i=4),
+                in0=src, in1=src, op=ALU.mult,
+            )
 
         def quantise(n):
             codes = mx_pool.tile([P, W], U32, align_bytes=64)

@@ -20,10 +20,13 @@ FLOPS = 2 * B * C * C * L
 PEDESTAL = 2.0 ** -36
 GAMMA_BOUND = 2.0 ** -18
 BETA_BOUND = (1e-6 + PEDESTAL) ** 0.5
-CA = (352, 96, 256, 328, 328, 328, 328, 328)
+X_TILES = ((0, 0, 512), (0, 512, 512), (0, 1024, 1024), (1, 0, 1024), (1, 1024, 1024))
+LOADS = (
+    ("g", 0), ("x", 0, 0, 256), ("g", 1), ("g", 2), ("g", 3), ("x", 0, 256, 256),
+    ("x", 1, 0, 512), ("x", 2, 0, 1024), ("x", 3, 0, 1024), ("x", 4, 0, 1024),
+)
+CA = (0, 384, 256, 352, 336, 320, 320, 320)
 SG = (2, 2, 2, 2, 2, 2, 1, 1)
-LOADS = ((0, 0, 512), (0, 512, 512), (0, 1024, 1024), (1, 0, 1024), (1, 1024, 1024))
-GAMMA_AFTER = 0
 
 
 def tile_gdn_1d_kernel(tc, x, beta_param, gamma_param, out):
@@ -38,26 +41,32 @@ def tile_gdn_1d_kernel(tc, x, beta_param, gamma_param, out):
 
         bp = const.tile([P, PACK], BF16)
         nc.scalar.dma_start(out=bp[:], in_=beta_param.rearrange("(p j) -> p j", j=PACK))
-        x_tiles = []
         g_sb = const.tile([P, PACK, C], BF16)
-        for i, (b, l0, width) in enumerate(LOADS):
-            xt = const.tile([P, PACK, width], BF16, name="x%d" % i)
-            nc.sync.dma_start(
-                out=xt[:],
-                in_=x[b].rearrange("(p j) l -> p j l", j=PACK)[:, :, l0 : l0 + width],
-            )
+        x_tiles = []
+        for k, (b, l0, width) in enumerate(X_TILES):
+            xt = const.tile([P, PACK, width], BF16, name="x%d" % k)
             x_tiles.append(xt)
-            if i == GAMMA_AFTER:
+        for load in LOADS:
+            if load[0] == "g":
+                j = load[1]
                 nc.sync.dma_start(
-                    out=g_sb[:], in_=gamma_param.rearrange("(m j) i -> m j i", j=PACK)
+                    out=g_sb[:, j, :],
+                    in_=gamma_param.rearrange("(m j) i -> m j i", j=PACK)[:, j, :],
+                )
+            else:
+                k, c0, width = load[1], load[2], load[3]
+                b, l0 = X_TILES[k][0], X_TILES[k][1] + c0
+                nc.sync.dma_start(
+                    out=x_tiles[k][:, :, c0 : c0 + width],
+                    in_=x[b].rearrange("(p j) l -> p j l", j=PACK)[:, :, l0 : l0 + width],
                 )
 
-        def x_block(n):
+        def x_chunk(n):
             b, l0 = n // (L // W), (n % (L // W)) * W
-            for i, (lb, ll0, width) in enumerate(LOADS):
-                if lb == b and ll0 <= l0 < ll0 + width:
-                    return x_tiles[i][:, :, l0 - ll0 : l0 - ll0 + W]
-            raise ValueError("no load holds block %d" % n)
+            for k, (tb, tl0, width) in enumerate(X_TILES):
+                if tb == b and tl0 <= l0 < tl0 + width:
+                    return x_tiles[k][:, :, l0 - tl0 : l0 - tl0 + W]
+            raise ValueError("no tile holds chunk %d" % n)
 
         ident = const.tile([P, P], F32)
         make_identity(nc, ident[:])
@@ -66,14 +75,16 @@ def tile_gdn_1d_kernel(tc, x, beta_param, gamma_param, out):
         warm = const.tile([P, 1], F32)
         nc.scalar.activation(out=warm[:], in_=one[:], func=ACT.Abs_reciprocal_sqrt)
 
-        bh = const.tile([P, PACK], F32)
-        nc.vector.tensor_scalar_max(out=bh[:], in0=bp[:], scalar1=BETA_BOUND)
-        bsq = const.tile([P, PACK], F32)
-        nc.vector.tensor_tensor(out=bsq[:], in0=bh[:], in1=bh[:], op=ALU.mult)
         beta = const.tile([P, PACK], F32)
-        nc.vector.tensor_scalar(
-            out=beta[:], in0=bsq[:], scalar1=PEDESTAL, scalar2=None, op0=ALU.subtract
-        )
+
+        def beta_values():
+            bh = const.tile([P, PACK], F32)
+            nc.vector.tensor_scalar_max(out=bh[:], in0=bp[:], scalar1=BETA_BOUND)
+            bsq = const.tile([P, PACK], F32)
+            nc.vector.tensor_tensor(out=bsq[:], in0=bh[:], in1=bh[:], op=ALU.mult)
+            nc.vector.tensor_scalar(
+                out=beta[:], in0=bsq[:], scalar1=PEDESTAL, scalar2=None, op0=ALU.subtract
+            )
 
         g_codes = const.tile([P, PACK, P], U32, align_bytes=64)
         g_scales = const.tile([P, PACK, P], U8, align_bytes=64)
@@ -82,16 +93,17 @@ def tile_gdn_1d_kernel(tc, x, beta_param, gamma_param, out):
         gam = const.tile([P, PACK, C], BF16, align_bytes=64)
         gts = {}
 
-        def gamma_floor():
-            nc.vector.tensor_scalar_max(out=h_sb[:], in0=g_sb[:], scalar1=GAMMA_BOUND)
+        def gamma_floor(j):
+            nc.vector.tensor_scalar_max(
+                out=h_sb[:, j, :], in0=g_sb[:, j, :], scalar1=GAMMA_BOUND
+            )
 
-        def gamma_transposes():
+        def gamma_transposes(j):
             hw = h_sb[:].bitcast(F32).rearrange("m j (p u) -> m j u p", u=2)
-            for j in range(PACK):
-                gt = psum.tile([P, 2, P], F32, tag="bank")
-                gts[j] = gt
-                for u in range(2):
-                    nc.tensor.transpose(gt[:, u, :], hw[:, j, u, :], ident[:])
+            gt = psum.tile([P, 2, P], F32, tag="bank")
+            gts[j] = gt
+            for u in range(2):
+                nc.tensor.transpose(gt[:, u, :], hw[:, j, u, :], ident[:])
 
         def gamma_square(j):
             nc.scalar.activation(
@@ -116,6 +128,7 @@ def tile_gdn_1d_kernel(tc, x, beta_param, gamma_param, out):
         grps = {}
         mxs = {}
         banks = {}
+        rs = {}
 
         def grp_tile(n):
             if n not in grps:
@@ -123,17 +136,17 @@ def tile_gdn_1d_kernel(tc, x, beta_param, gamma_param, out):
                 grps[n] = grp
             return grps[n]
 
-        def squares_act(n):
+        def squares_act(n, c0, c1):
             nc.scalar.activation(
-                out=grp_tile(n)[:, 0 : CA[n], :].rearrange("p (c i) t -> p c t i", i=4),
-                in_=x_block(n)[:, :, 0 : CA[n]].rearrange("p t (c i) -> p c t i", i=4),
+                out=grp_tile(n)[:, c0:c1, :].rearrange("p (c i) t -> p c t i", i=4),
+                in_=x_chunk(n)[:, :, c0:c1].rearrange("p t (c i) -> p c t i", i=4),
                 func=ACT.Square,
             )
 
-        def squares_dve(n):
-            src = x_block(n)[:, :, CA[n] : W].rearrange("p t (c i) -> p c t i", i=4)
+        def squares_dve(n, c0, c1):
+            src = x_chunk(n)[:, :, c0:c1].rearrange("p t (c i) -> p c t i", i=4)
             nc.vector.tensor_tensor(
-                out=grp_tile(n)[:, CA[n] : W, :].rearrange("p (c i) t -> p c t i", i=4),
+                out=grp_tile(n)[:, c0:c1, :].rearrange("p (c i) t -> p c t i", i=4),
                 in0=src, in1=src, op=ALU.mult,
             )
 
@@ -162,52 +175,62 @@ def tile_gdn_1d_kernel(tc, x, beta_param, gamma_param, out):
                     stop=True,
                 )
 
-        def epilogue(n):
-            xs = x_block(n)
-            b, l0 = n // (L // W), (n % (L // W)) * W
-            out_v = out[b].rearrange("(p j) l -> p j l", j=PACK)[:, :, l0 : l0 + W]
+        def rsqrts(n):
             r = r_pool.tile([P, PACK, W], F32)
-            sg = SG[n]
-            mg = min(sg, 2)
+            rs[n] = r
             for j in range(PACK):
                 nc.scalar.activation(
                     out=r[:, j, :], in_=banks[(n, j)][:], func=ACT.Abs_reciprocal_sqrt,
                     bias=beta[:, j : j + 1], scale=1.0,
                 )
-                if (j + 1) % mg == 0:
-                    js = slice(j + 1 - mg, j + 1)
-                    nc.vector.tensor_tensor(
-                        out=r[:, js, :], in0=r[:, js, :], in1=xs[:, js, :], op=ALU.mult
-                    )
-                if (j + 1) % sg == 0:
-                    js = slice(j + 1 - sg, j + 1)
-                    nc.sync.dma_start(out=out_v[:, js, :], in_=r[:, js, :])
 
-        squares_act(0)
-        squares_dve(0)
-        gamma_floor()
-        gamma_transposes()
-        quantise(0)
-        squares_dve(1)
-        gamma_square(0)
-        gamma_square(1)
+        def products_and_stores(n):
+            xs = x_chunk(n)
+            r = rs[n]
+            b, l0 = n // (L // W), (n % (L // W)) * W
+            out_v = out[b].rearrange("(p j) l -> p j l", j=PACK)[:, :, l0 : l0 + W]
+            for j0 in range(0, PACK, SG[n]):
+                js = slice(j0, j0 + SG[n])
+                nc.vector.tensor_tensor(
+                    out=r[:, js, :], in0=r[:, js, :], in1=xs[:, js, :], op=ALU.mult
+                )
+                nc.sync.dma_start(out=out_v[:, js, :], in_=r[:, js, :])
+
+        gamma_floor(0)
+        gamma_transposes(0)
+        beta_values()
+        squares_act(0, 0, 144)
+        gamma_floor(1)
+        gamma_transposes(1)
+        squares_dve(0, 144, 256)
+        gamma_floor(2)
+        gamma_transposes(2)
+        gamma_floor(3)
+        gamma_transposes(3)
+        for j in range(PACK):
+            gamma_square(j)
         gamma_round(0)
+        squares_dve(0, 400, 512)
         gamma_round(1)
         gamma_quantise(0)
-        gamma_square(2)
         gamma_round(2)
         gamma_quantise(1)
-        gamma_square(3)
         gamma_round(3)
         gamma_quantise(2)
         gamma_quantise(3)
-        squares_act(1)
+        squares_act(0, 256, 400)
+        quantise(0)
         matmuls(0)
-        for s in range(2, NB + 2):
-            if s < NB:
-                squares_act(s)
-                squares_dve(s)
-            if s <= NB:
-                quantise(s - 1)
-                matmuls(s - 1)
-            epilogue(s - 2)
+        squares_act(1, 0, CA[1])
+        squares_dve(1, CA[1], W)
+        for n in range(NB):
+            if n + 2 < NB:
+                squares_dve(n + 2, CA[n + 2], W)
+            if n + 1 < NB:
+                quantise(n + 1)
+            rsqrts(n)
+            if n + 1 < NB:
+                matmuls(n + 1)
+            if n + 2 < NB:
+                squares_act(n + 2, 0, CA[n + 2])
+            products_and_stores(n)

@@ -23,9 +23,9 @@ BETA_BOUND = (1e-6 + PEDESTAL) ** 0.5
 X_TILES = ((0, 0, 512), (0, 512, 512), (0, 1024, 1024), (1, 0, 1024), (1, 1024, 1024))
 LOADS = (
     ("g", 0), ("x", 0, 0, 256), ("g", 1), ("g", 2), ("g", 3), ("x", 0, 256, 256),
-    ("x", 1, 0, 512), ("x", 2, 0, 1024), ("x", 3, 0, 1024), ("x", 4, 0, 1024),
+    ("x", 1, 0, 512), ("x", 2, 0, 512), ("x", 2, 512, 512), ("x", 3, 0, 1024), ("x", 4, 0, 1024),
 )
-CA = (0, 384, 256, 352, 336, 320, 320, 320)
+CA = (0, 432, 192, 376, 336, 320, 352, 320)
 SG = (2, 2, 2, 2, 2, 2, 1, 1)
 
 
@@ -210,7 +210,7 @@ def tile_gdn_1d_kernel(tc, x, beta_param, gamma_param, out):
         for j in range(PACK):
             gamma_square(j)
         gamma_round(0)
-        squares_dve(0, 400, 512)
+        squares_dve(0, 408, 512)
         gamma_round(1)
         gamma_quantise(0)
         gamma_round(2)
@@ -218,7 +218,7 @@ def tile_gdn_1d_kernel(tc, x, beta_param, gamma_param, out):
         gamma_round(3)
         gamma_quantise(2)
         gamma_quantise(3)
-        squares_act(0, 256, 400)
+        squares_act(0, 256, 408)
         quantise(0)
         matmuls(0)
         squares_act(1, 0, CA[1])

@@ -16,6 +16,7 @@ P = 128
 PACK = 4
 W = 512
 NB = B * L // W
+RUN = 8
 FLOPS = 2 * B * C * C * L
 PEDESTAL = 2.0 ** -36
 GAMMA_BOUND = 2.0 ** -18
@@ -138,15 +139,15 @@ def tile_gdn_1d_kernel(tc, x, beta_param, gamma_param, out):
 
         def squares_act(n, c0, c1):
             nc.scalar.activation(
-                out=grp_tile(n)[:, c0:c1, :].rearrange("p (c i) t -> p c t i", i=4),
-                in_=x_chunk(n)[:, :, c0:c1].rearrange("p t (c i) -> p c t i", i=4),
+                out=grp_tile(n)[:, c0:c1, :].rearrange("p (c i) t -> p c t i", i=RUN),
+                in_=x_chunk(n)[:, :, c0:c1].rearrange("p t (c i) -> p c t i", i=RUN),
                 func=ACT.Square,
             )
 
         def squares_dve(n, c0, c1):
-            src = x_chunk(n)[:, :, c0:c1].rearrange("p t (c i) -> p c t i", i=4)
+            src = x_chunk(n)[:, :, c0:c1].rearrange("p t (c i) -> p c t i", i=RUN)
             nc.vector.tensor_tensor(
-                out=grp_tile(n)[:, c0:c1, :].rearrange("p (c i) t -> p c t i", i=4),
+                out=grp_tile(n)[:, c0:c1, :].rearrange("p (c i) t -> p c t i", i=RUN),
                 in0=src, in1=src, op=ALU.mult,
             )
 

@@ -26,8 +26,9 @@ LOADS = (
     ("g", 0), ("x", 0, 0, 256), ("g", 1), ("g", 2), ("g", 3), ("x", 0, 256, 256),
     ("x", 1, 0, 512), ("x", 2, 0, 512), ("x", 2, 512, 512), ("x", 3, 0, 1024), ("x", 4, 0, 1024),
 )
-CA = (0, 432, 192, 376, 336, 320, 352, 320)
+CA = (0, 432, 192, 312, 272, 256, 288, 320)
 SG = (2, 2, 2, 2, 2, 2, 1, 1)
+WINDOWS = (1, 2, 3, 4)
 
 
 def tile_gdn_1d_kernel(tc, x, beta_param, gamma_param, out):
@@ -37,7 +38,8 @@ def tile_gdn_1d_kernel(tc, x, beta_param, gamma_param, out):
         grp_pool = ctx.enter_context(tc.tile_pool(name="grp", bufs=3))
         mx_pool = ctx.enter_context(tc.tile_pool(name="mx", bufs=3))
         r_pool = ctx.enter_context(tc.tile_pool(name="r", bufs=4))
-        psum = ctx.enter_context(tc.psum_pool(name="psum", bufs=8))
+        psum = ctx.enter_context(tc.psum_pool(name="psum", bufs=4))
+        psum_x = ctx.enter_context(tc.psum_pool(name="psum_x", bufs=4))
         ctx.enter_context(tc.manual_schedule())
 
         bp = const.tile([P, PACK], BF16)
@@ -71,6 +73,9 @@ def tile_gdn_1d_kernel(tc, x, beta_param, gamma_param, out):
 
         ident = const.tile([P, P], F32)
         make_identity(nc, ident[:])
+        ident_bf = const.tile([P, P], BF16)
+        make_identity(nc, ident_bf[:])
+        seen = const.tile([P, 1], U32)
         one = const.tile([P, 1], F32)
         nc.vector.memset(one[:], 1.0)
         warm = const.tile([P, 1], F32)
@@ -185,17 +190,55 @@ def tile_gdn_1d_kernel(tc, x, beta_param, gamma_param, out):
                     bias=beta[:, j : j + 1], scale=1.0,
                 )
 
+        def out_chunk(n):
+            b, l0 = n // (L // W), (n % (L // W)) * W
+            return out[b].rearrange("(p j) l -> p j l", j=PACK)[:, :, l0 : l0 + W]
+
+        xps = {}
+
+        def x_to_psum(n):
+            xs = x_chunk(n)
+            pair = psum_x.tile([P, 2, W], BF16, tag="xp")
+            single = psum_x.tile([P, 2, W], BF16, tag="xp")
+            xps[n] = (pair, single)
+            for j in range(3):
+                nc.tensor.matmul(
+                    xps[n][j // 2][:, j % 2, :], lhsT=ident_bf[:], rhs=xs[:, j, :],
+                    start=True, stop=True,
+                )
+
+        def gpsimd_product(n, after):
+            nc.gpsimd.tensor_copy(out=seen[:], in_=mxs[after][0][:, 0:1])
+            r = rs[n]
+            nc.gpsimd.tensor_tensor(
+                out=r[:, 3, :], in0=r[:, 3, :], in1=x_chunk(n)[:, 3, :], op=ALU.mult
+            )
+
         def products_and_stores(n):
             xs = x_chunk(n)
             r = rs[n]
-            b, l0 = n // (L // W), (n % (L // W)) * W
-            out_v = out[b].rearrange("(p j) l -> p j l", j=PACK)[:, :, l0 : l0 + W]
-            for j0 in range(0, PACK, SG[n]):
-                js = slice(j0, j0 + SG[n])
+            out_v = out_chunk(n)
+            if n in WINDOWS:
+                pair, single = xps[n]
                 nc.vector.tensor_tensor(
-                    out=r[:, js, :], in0=r[:, js, :], in1=xs[:, js, :], op=ALU.mult
+                    out=r[:, 0:2, :], in0=r[:, 0:2, :], in1=pair[:], op=ALU.mult
                 )
-                nc.sync.dma_start(out=out_v[:, js, :], in_=r[:, js, :])
+                nc.sync.dma_start(out=out_v[:, 0:2, :], in_=r[:, 0:2, :])
+                nc.vector.tensor_tensor(
+                    out=r[:, 2, :], in0=r[:, 2, :], in1=single[:, 0, :], op=ALU.mult
+                )
+                nc.sync.dma_start(out=out_v[:, 2, :], in_=r[:, 2, :])
+                nc.sync.dma_start(out=out_chunk(n - 1)[:, 3, :], in_=rs[n - 1][:, 3, :])
+                groups = () if n + 1 in WINDOWS else ((3, 4),)
+            elif n + 1 in WINDOWS:
+                groups = ((0, 2), (2, 3))
+            else:
+                groups = tuple((j0, j0 + SG[n]) for j0 in range(0, PACK, SG[n]))
+            for j0, j1 in groups:
+                nc.vector.tensor_tensor(
+                    out=r[:, j0:j1, :], in0=r[:, j0:j1, :], in1=xs[:, j0:j1, :], op=ALU.mult
+                )
+                nc.sync.dma_start(out=out_v[:, j0:j1, :], in_=r[:, j0:j1, :])
 
         gamma_floor(0)
         gamma_transposes(0)
@@ -229,7 +272,11 @@ def tile_gdn_1d_kernel(tc, x, beta_param, gamma_param, out):
                 squares_dve(n + 2, CA[n + 2], W)
             if n + 1 < NB:
                 quantise(n + 1)
+            if n in WINDOWS:
+                gpsimd_product(n - 1, n + 1)
             rsqrts(n)
+            if n + 1 in WINDOWS:
+                x_to_psum(n + 1)
             if n + 1 < NB:
                 matmuls(n + 1)
             if n + 2 < NB:

@@ -75,7 +75,7 @@ def tile_gdn_1d_kernel(tc, x, beta_param, gamma_param, out):
         make_identity(nc, ident[:])
         ident_bf = const.tile([P, P], BF16)
         make_identity(nc, ident_bf[:])
-        seen = const.tile([P, 1], U32)
+        seen = const.tile([P, 2], BF16)
         one = const.tile([P, 1], F32)
         nc.vector.memset(one[:], 1.0)
         warm = const.tile([P, 1], F32)
@@ -208,7 +208,7 @@ def tile_gdn_1d_kernel(tc, x, beta_param, gamma_param, out):
                 )
 
         def gpsimd_product(n, after):
-            nc.gpsimd.tensor_copy(out=seen[:], in_=mxs[after][0][:, 0:1])
+            nc.gpsimd.tensor_copy(out=seen[:], in_=grps[after][:, W - 1, 0:2])
             r = rs[n]
             nc.gpsimd.tensor_tensor(
                 out=r[:, 3, :], in0=r[:, 3, :], in1=x_chunk(n)[:, 3, :], op=ALU.mult
@@ -270,10 +270,10 @@ def tile_gdn_1d_kernel(tc, x, beta_param, gamma_param, out):
         for n in range(NB):
             if n + 2 < NB:
                 squares_dve(n + 2, CA[n + 2], W)
+            if n in WINDOWS:
+                gpsimd_product(n - 1, n + 2)
             if n + 1 < NB:
                 quantise(n + 1)
-            if n in WINDOWS:
-                gpsimd_product(n - 1, n + 1)
             rsqrts(n)
             if n + 1 in WINDOWS:
                 x_to_psum(n + 1)

@@ -23,11 +23,12 @@ GAMMA_BOUND = 2.0 ** -18
 BETA_BOUND = (1e-6 + PEDESTAL) ** 0.5
 X_TILES = ((0, 0, 512), (0, 512, 512), (0, 1024, 1024), (1, 0, 1024), (1, 1024, 1024))
 LOADS = (
-    ("g", 0), ("x", 0, 0, 256), ("g", 1), ("g", 2), ("g", 3), ("x", 0, 256, 256),
+    ("g", 0), ("g", 1), ("x", 0, 0, 256), ("g", 2), ("g", 3), ("x", 0, 256, 256),
     ("x", 1, 0, 512), ("x", 2, 0, 512), ("x", 2, 512, 512), ("x", 3, 0, 1024), ("x", 4, 0, 1024),
 )
 CA = (0, 432, 192, 312, 272, 256, 288, 320)
 SG = (2, 2, 2, 2, 2, 2, 1, 1)
+LAST_CUTS = (0, 256, 512)
 WINDOWS = (1, 2, 3, 4)
 
 
@@ -185,10 +186,12 @@ def tile_gdn_1d_kernel(tc, x, beta_param, gamma_param, out):
             r = r_pool.tile([P, PACK, W], F32)
             rs[n] = r
             for j in range(PACK):
-                nc.scalar.activation(
-                    out=r[:, j, :], in_=banks[(n, j)][:], func=ACT.Abs_reciprocal_sqrt,
-                    bias=beta[:, j : j + 1], scale=1.0,
-                )
+                cuts = LAST_CUTS if (n, j) == (NB - 1, PACK - 1) else (0, W)
+                for c0, c1 in zip(cuts[:-1], cuts[1:]):
+                    nc.scalar.activation(
+                        out=r[:, j, c0:c1], in_=banks[(n, j)][:, c0:c1],
+                        func=ACT.Abs_reciprocal_sqrt, bias=beta[:, j : j + 1], scale=1.0,
+                    )
 
         def out_chunk(n):
             b, l0 = n // (L // W), (n % (L // W)) * W
@@ -235,10 +238,13 @@ def tile_gdn_1d_kernel(tc, x, beta_param, gamma_param, out):
             else:
                 groups = tuple((j0, j0 + SG[n]) for j0 in range(0, PACK, SG[n]))
             for j0, j1 in groups:
-                nc.vector.tensor_tensor(
-                    out=r[:, j0:j1, :], in0=r[:, j0:j1, :], in1=xs[:, j0:j1, :], op=ALU.mult
-                )
-                nc.sync.dma_start(out=out_v[:, j0:j1, :], in_=r[:, j0:j1, :])
+                cuts = LAST_CUTS if (n, j0) == (NB - 1, PACK - 1) else (0, W)
+                for c0, c1 in zip(cuts[:-1], cuts[1:]):
+                    nc.vector.tensor_tensor(
+                        out=r[:, j0:j1, c0:c1], in0=r[:, j0:j1, c0:c1], in1=xs[:, j0:j1, c0:c1],
+                        op=ALU.mult,
+                    )
+                    nc.sync.dma_start(out=out_v[:, j0:j1, c0:c1], in_=r[:, j0:j1, c0:c1])
 
         gamma_floor(0)
         gamma_transposes(0)

@@ -26,7 +26,7 @@ LOADS = (
     ("g", 0), ("g", 1), ("x", 0, 0, 256), ("g", 2), ("g", 3), ("x", 0, 256, 256),
     ("x", 1, 0, 512), ("x", 2, 0, 512), ("x", 2, 512, 512), ("x", 3, 0, 1024), ("x", 4, 0, 1024),
 )
-CA = (0, 432, 192, 312, 272, 256, 288, 320)
+CA = (0, 432, 192, 296, 256, 240, 272, 320)
 SG = (2, 2, 2, 2, 2, 2, 1, 1)
 LAST_CUTS = (0, 256, 512)
 WINDOWS = (1, 2, 3, 4)

@@ -36,9 +36,9 @@ def tile_gdn_1d_kernel(tc, x, beta_param, gamma_param, out):
     nc = tc.nc
     with ExitStack() as ctx:
         const = ctx.enter_context(tc.tile_pool(name="const", bufs=1))
-        grp_pool = ctx.enter_context(tc.tile_pool(name="grp", bufs=3))
-        mx_pool = ctx.enter_context(tc.tile_pool(name="mx", bufs=3))
-        r_pool = ctx.enter_context(tc.tile_pool(name="r", bufs=4))
+        grp_pool = ctx.enter_context(tc.tile_pool(name="grp", bufs=NB))
+        mx_pool = ctx.enter_context(tc.tile_pool(name="mx", bufs=NB))
+        r_pool = ctx.enter_context(tc.tile_pool(name="r", bufs=NB))
         psum = ctx.enter_context(tc.psum_pool(name="psum", bufs=4))
         psum_x = ctx.enter_context(tc.psum_pool(name="psum_x", bufs=4))
         ctx.enter_context(tc.manual_schedule())

@@ -76,7 +76,6 @@ def tile_gdn_1d_kernel(tc, x, beta_param, gamma_param, out):
         make_identity(nc, ident[:])
         ident_bf = const.tile([P, P], BF16)
         make_identity(nc, ident_bf[:])
-        seen = const.tile([P, 2], BF16)
         one = const.tile([P, 1], F32)
         nc.vector.memset(one[:], 1.0)
         warm = const.tile([P, 1], F32)
@@ -210,11 +209,13 @@ def tile_gdn_1d_kernel(tc, x, beta_param, gamma_param, out):
                     start=True, stop=True,
                 )
 
-        def gpsimd_product(n, after):
-            nc.gpsimd.tensor_copy(out=seen[:], in_=grps[after][:, W - 1, 0:2])
-            r = rs[n]
+        def gpsimd_out(n):
+            flat = grps[n + 2][:].rearrange("p w t -> p (w t)").bitcast(F32)
+            return flat[:, 0:W]
+
+        def gpsimd_product(n):
             nc.gpsimd.tensor_tensor(
-                out=r[:, 3, :], in0=r[:, 3, :], in1=x_chunk(n)[:, 3, :], op=ALU.mult
+                out=gpsimd_out(n), in0=rs[n][:, 3, :], in1=x_chunk(n)[:, 3, :], op=ALU.mult
             )
 
         def products_and_stores(n):
@@ -231,7 +232,7 @@ def tile_gdn_1d_kernel(tc, x, beta_param, gamma_param, out):
                     out=r[:, 2, :], in0=r[:, 2, :], in1=single[:, 0, :], op=ALU.mult
                 )
                 nc.sync.dma_start(out=out_v[:, 2, :], in_=r[:, 2, :])
-                nc.sync.dma_start(out=out_chunk(n - 1)[:, 3, :], in_=rs[n - 1][:, 3, :])
+                nc.sync.dma_start(out=out_chunk(n - 1)[:, 3, :], in_=gpsimd_out(n - 1))
                 groups = () if n + 1 in WINDOWS else ((3, 4),)
             elif n + 1 in WINDOWS:
                 groups = ((0, 2), (2, 3))
@@ -276,10 +277,10 @@ def tile_gdn_1d_kernel(tc, x, beta_param, gamma_param, out):
         for n in range(NB):
             if n + 2 < NB:
                 squares_dve(n + 2, CA[n + 2], W)
-            if n in WINDOWS:
-                gpsimd_product(n - 1, n + 2)
             if n + 1 < NB:
                 quantise(n + 1)
+            if n in WINDOWS:
+                gpsimd_product(n - 1)
             rsqrts(n)
             if n + 1 in WINDOWS:
                 x_to_psum(n + 1)

@@ -24,7 +24,7 @@ BETA_BOUND = (1e-6 + PEDESTAL) ** 0.5
 X_TILES = ((0, 0, 512), (0, 512, 512), (0, 1024, 1024), (1, 0, 1024), (1, 1024, 1024))
 LOADS = (
     ("g", 0), ("g", 1), ("x", 0, 0, 256), ("g", 2), ("g", 3), ("x", 0, 256, 256),
-    ("x", 1, 0, 512), ("x", 2, 0, 512), ("x", 2, 512, 512), ("x", 3, 0, 1024), ("x", 4, 0, 1024),
+    ("b",), ("x", 1, 0, 512), ("x", 2, 0, 512), ("x", 2, 512, 512), ("x", 3, 0, 1024), ("x", 4, 0, 1024),
 )
 CA = (0, 432, 192, 296, 256, 240, 272, 320)
 SG = (2, 2, 2, 2, 2, 2, 1, 1)
@@ -44,7 +44,6 @@ def tile_gdn_1d_kernel(tc, x, beta_param, gamma_param, out):
         ctx.enter_context(tc.manual_schedule())
 
         bp = const.tile([P, PACK], BF16)
-        nc.scalar.dma_start(out=bp[:], in_=beta_param.rearrange("(p j) -> p j", j=PACK))
         g_sb = const.tile([P, PACK, C], BF16)
         x_tiles = []
         for k, (b, l0, width) in enumerate(X_TILES):
@@ -57,6 +56,8 @@ def tile_gdn_1d_kernel(tc, x, beta_param, gamma_param, out):
                     out=g_sb[:, j, :],
                     in_=gamma_param.rearrange("(m j) i -> m j i", j=PACK)[:, j, :],
                 )
+            elif load[0] == "b":
+                nc.sync.dma_start(out=bp[:], in_=beta_param.rearrange("(p j) -> p j", j=PACK))
             else:
                 k, c0, width = load[1], load[2], load[3]
                 b, l0 = X_TILES[k][0], X_TILES[k][1] + c0
@@ -249,7 +250,6 @@ def tile_gdn_1d_kernel(tc, x, beta_param, gamma_param, out):
 
         gamma_floor(0)
         gamma_transposes(0)
-        beta_values()
         squares_act(0, 0, 144)
         gamma_floor(1)
         gamma_transposes(1)
@@ -269,6 +269,7 @@ def tile_gdn_1d_kernel(tc, x, beta_param, gamma_param, out):
         gamma_round(3)
         gamma_quantise(2)
         gamma_quantise(3)
+        beta_values()
         squares_act(0, 256, 408)
         quantise(0)
         matmuls(0)

@@ -23,8 +23,8 @@ GAMMA_BOUND = 2.0 ** -18
 BETA_BOUND = (1e-6 + PEDESTAL) ** 0.5
 X_TILES = ((0, 0, 512), (0, 512, 512), (0, 1024, 1024), (1, 0, 1024), (1, 1024, 1024))
 LOADS = (
-    ("g", 0), ("g", 1), ("x", 0, 0, 256), ("g", 2), ("g", 3), ("x", 0, 256, 256),
-    ("b",), ("x", 1, 0, 512), ("x", 2, 0, 512), ("x", 2, 512, 512), ("x", 3, 0, 1024), ("x", 4, 0, 1024),
+    ("g", 0), ("g", 1), ("x", 0, 0, 256), ("g", 2), ("g", 3), ("b",), ("x", 0, 256, 256),
+    ("x", 1, 0, 512), ("x", 2, 0, 512), ("x", 2, 512, 512), ("x", 3, 0, 1024), ("x", 4, 0, 1024),
 )
 CA = (0, 432, 192, 296, 256, 240, 272, 320)
 SG = (2, 2, 2, 2, 2, 2, 1, 1)
@@ -258,6 +258,7 @@ def tile_gdn_1d_kernel(tc, x, beta_param, gamma_param, out):
         gamma_transposes(2)
         gamma_floor(3)
         gamma_transposes(3)
+        beta_values()
         for j in range(PACK):
             gamma_square(j)
         gamma_round(0)
@@ -269,7 +270,6 @@ def tile_gdn_1d_kernel(tc, x, beta_param, gamma_param, out):
         gamma_round(3)
         gamma_quantise(2)
         gamma_quantise(3)
-        beta_values()
         squares_act(0, 256, 408)
         quantise(0)
         matmuls(0)

@@ -26,7 +26,7 @@ LOADS = (
     ("g", 0), ("g", 1), ("x", 0, 0, 256), ("g", 2), ("g", 3), ("b",), ("x", 0, 256, 256),
     ("x", 1, 0, 512), ("x", 2, 0, 512), ("x", 2, 512, 512), ("x", 3, 0, 1024), ("x", 4, 0, 1024),
 )
-CA = (0, 432, 192, 296, 256, 240, 272, 320)
+CA = (0, 432, 192, 296, 256, 240, 304, 360)
 SG = (2, 2, 2, 2, 2, 2, 1, 1)
 LAST_CUTS = (0, 256, 512)
 WINDOWS = (1, 2, 3, 4)

@@ -23,8 +23,8 @@ GAMMA_BOUND = 2.0 ** -18
 BETA_BOUND = (1e-6 + PEDESTAL) ** 0.5
 X_TILES = ((0, 0, 512), (0, 512, 512), (0, 1024, 1024), (1, 0, 1024), (1, 1024, 1024))
 LOADS = (
-    ("g", 0), ("g", 1), ("x", 0, 0, 256), ("g", 2), ("g", 3), ("b",), ("x", 0, 256, 256),
-    ("x", 1, 0, 512), ("x", 2, 0, 512), ("x", 2, 512, 512), ("x", 3, 0, 1024), ("x", 4, 0, 1024),
+    ("g", 0), ("g", 1), ("x", 0, 0, 256), ("g", 2), ("g", 3), ("x", 0, 256, 256),
+    ("b",), ("x", 1, 0, 512), ("x", 2, 0, 512), ("x", 2, 512, 512), ("x", 3, 0, 1024), ("x", 4, 0, 1024),
 )
 CA = (0, 432, 192, 296, 256, 240, 304, 360)
 SG = (2, 2, 2, 2, 2, 2, 1, 1)
@@ -84,11 +84,16 @@ def tile_gdn_1d_kernel(tc, x, beta_param, gamma_param, out):
 
         beta = const.tile([P, PACK], F32)
 
-        def beta_values():
-            bh = const.tile([P, PACK], F32)
+        bh = const.tile([P, PACK], F32)
+        bsq = const.tile([P, PACK], F32)
+
+        def beta_floor():
             nc.vector.tensor_scalar_max(out=bh[:], in0=bp[:], scalar1=BETA_BOUND)
-            bsq = const.tile([P, PACK], F32)
+
+        def beta_square():
             nc.vector.tensor_tensor(out=bsq[:], in0=bh[:], in1=bh[:], op=ALU.mult)
+
+        def beta_less_pedestal():
             nc.vector.tensor_scalar(
                 out=beta[:], in0=bsq[:], scalar1=PEDESTAL, scalar2=None, op0=ALU.subtract
             )
@@ -258,7 +263,6 @@ def tile_gdn_1d_kernel(tc, x, beta_param, gamma_param, out):
         gamma_transposes(2)
         gamma_floor(3)
         gamma_transposes(3)
-        beta_values()
         for j in range(PACK):
             gamma_square(j)
         gamma_round(0)
@@ -267,11 +271,14 @@ def tile_gdn_1d_kernel(tc, x, beta_param, gamma_param, out):
         gamma_quantise(0)
         gamma_round(2)
         gamma_quantise(1)
+        beta_floor()
         gamma_round(3)
         gamma_quantise(2)
+        beta_square()
         gamma_quantise(3)
         squares_act(0, 256, 408)
         quantise(0)
+        beta_less_pedestal()
         matmuls(0)
         squares_act(1, 0, CA[1])
         squares_dve(1, CA[1], W)

from contextlib import ExitStack

import concourse.mybir as mybir
from concourse.masks import make_identity

F32 = mybir.dt.float32
BF16 = mybir.dt.bfloat16
U32 = mybir.dt.uint32
U8 = mybir.dt.uint8
FP8X4 = mybir.dt.float8_e4m3fn_x4
ACT = mybir.ActivationFunctionType
ALU = mybir.AluOpType

B, C, L = 2, 512, 2048
P = 128
PACK = 4
W = 512
NB = B * L // W
RUN = 8
FLOPS = 2 * B * C * C * L
PEDESTAL = 2.0 ** -36
GAMMA_BOUND = 2.0 ** -18
BETA_BOUND = (1e-6 + PEDESTAL) ** 0.5
X_TILES = ((0, 0, 512), (0, 512, 512), (0, 1024, 1024), (1, 0, 1024), (1, 1024, 1024))
LOADS = (
    ("g", 0), ("g", 1), ("x", 0, 0, 256), ("g", 2), ("g", 3), ("x", 0, 256, 256),
    ("b",), ("x", 1, 0, 512), ("x", 2, 0, 512), ("x", 2, 512, 512), ("x", 3, 0, 1024), ("x", 4, 0, 1024),
)
CA = (0, 432, 192, 296, 256, 240, 304, 360)
SG = (2, 2, 2, 2, 2, 2, 1, 1)
LAST_CUTS = (0, 256, 512)
WINDOWS = (1, 2, 3, 4)


def tile_gdn_1d_kernel(tc, x, beta_param, gamma_param, out):
    nc = tc.nc
    with ExitStack() as ctx:
        const = ctx.enter_context(tc.tile_pool(name="const", bufs=1))
        grp_pool = ctx.enter_context(tc.tile_pool(name="grp", bufs=NB))
        mx_pool = ctx.enter_context(tc.tile_pool(name="mx", bufs=NB))
        r_pool = ctx.enter_context(tc.tile_pool(name="r", bufs=NB))
        psum = ctx.enter_context(tc.psum_pool(name="psum", bufs=4))
        psum_x = ctx.enter_context(tc.psum_pool(name="psum_x", bufs=4))
        ctx.enter_context(tc.manual_schedule())

        bp = const.tile([P, PACK], BF16)
        g_sb = const.tile([P, PACK, C], BF16)
        x_tiles = []
        for k, (b, l0, width) in enumerate(X_TILES):
            xt = const.tile([P, PACK, width], BF16, name="x%d" % k)
            x_tiles.append(xt)
        for load in LOADS:
            if load[0] == "g":
                j = load[1]
                nc.sync.dma_start(
                    out=g_sb[:, j, :],
                    in_=gamma_param.rearrange("(m j) i -> m j i", j=PACK)[:, j, :],
                )
            elif load[0] == "b":
                nc.sync.dma_start(out=bp[:], in_=beta_param.rearrange("(p j) -> p j", j=PACK))
            else:
                k, c0, width = load[1], load[2], load[3]
                b, l0 = X_TILES[k][0], X_TILES[k][1] + c0
                nc.sync.dma_start(
                    out=x_tiles[k][:, :, c0 : c0 + width],
                    in_=x[b].rearrange("(p j) l -> p j l", j=PACK)[:, :, l0 : l0 + width],
                )

        def x_chunk(n):
            b, l0 = n // (L // W), (n % (L // W)) * W
            for k, (tb, tl0, width) in enumerate(X_TILES):
                if tb == b and tl0 <= l0 < tl0 + width:
                    return x_tiles[k][:, :, l0 - tl0 : l0 - tl0 + W]
            raise ValueError("no tile holds chunk %d" % n)

        ident = const.tile([P, P], F32)
        make_identity(nc, ident[:])
        ident_bf = const.tile([P, P], BF16)
        make_identity(nc, ident_bf[:])
        one = const.tile([P, 1], F32)
        nc.vector.memset(one[:], 1.0)
        warm = const.tile([P, 1], F32)
        nc.scalar.activation(out=warm[:], in_=one[:], func=ACT.Abs_reciprocal_sqrt)

        beta = const.tile([P, PACK], F32)

        bh = const.tile([P, PACK], F32)
        bsq = const.tile([P, PACK], F32)

        def beta_floor():
            nc.vector.tensor_scalar_max(out=bh[:], in0=bp[:], scalar1=BETA_BOUND)

        def beta_square():
            nc.vector.tensor_tensor(out=bsq[:], in0=bh[:], in1=bh[:], op=ALU.mult)

        def beta_less_pedestal():
            nc.vector.tensor_scalar(
                out=beta[:], in0=bsq[:], scalar1=PEDESTAL, scalar2=None, op0=ALU.subtract
            )

        g_codes = const.tile([P, PACK, P], U32, align_bytes=64)
        g_scales = const.tile([P, PACK, P], U8, align_bytes=64)
        h_sb = const.tile([P, PACK, C], BF16)
        sq = const.tile([P, PACK, C], F32)
        gam = const.tile([P, PACK, C], BF16, align_bytes=64)
        gts = {}

        def gamma_floor(j):
            nc.vector.tensor_scalar_max(
                out=h_sb[:, j, :], in0=g_sb[:, j, :], scalar1=GAMMA_BOUND
            )

        def gamma_transposes(j):
            hw = h_sb[:].bitcast(F32).rearrange("m j (p u) -> m j u p", u=2)
            gt = psum.tile([P, 2, P], F32, tag="bank")
            gts[j] = gt
            for u in range(2):
                nc.tensor.transpose(gt[:, u, :], hw[:, j, u, :], ident[:])

        def gamma_square(j):
            nc.scalar.activation(
                out=sq[:, j, :].rearrange("p (m u e) -> p m u e", u=2, e=2),
                in_=gts[j][:].bitcast(BF16).rearrange("p u (m e) -> p m u e", e=2),
                func=ACT.Square,
            )

        def gamma_round(j):
            nc.vector.tensor_scalar(
                out=gam[:, j, :], in0=sq[:, j, :], scalar1=PEDESTAL, scalar2=None,
                op0=ALU.subtract,
            )

        def gamma_quantise(j):
            nc.vector.quantize_mx(
                out=g_codes[:, j, :].bitcast(FP8X4),
                scales=g_scales[:, j, :],
                in_=gam[:, j, :],
            )

        grps = {}
        mxs = {}
        banks = {}
        rs = {}

        def grp_tile(n):
            if n not in grps:
                grp = grp_pool.tile([P, W, PACK], BF16, align_bytes=64)
                grps[n] = grp
            return grps[n]

        def squares_act(n, c0, c1):
            nc.scalar.activation(
                out=grp_tile(n)[:, c0:c1, :].rearrange("p (c i) t -> p c t i", i=RUN),
                in_=x_chunk(n)[:, :, c0:c1].rearrange("p t (c i) -> p c t i", i=RUN),
                func=ACT.Square,
            )

        def squares_dve(n, c0, c1):
            src = x_chunk(n)[:, :, c0:c1].rearrange("p t (c i) -> p c t i", i=RUN)
            nc.vector.tensor_tensor(
                out=grp_tile(n)[:, c0:c1, :].rearrange("p (c i) t -> p c t i", i=RUN),
                in0=src, in1=src, op=ALU.mult,
            )

        def quantise(n):
            codes = mx_pool.tile([P, W], U32, align_bytes=64)
            scales = mx_pool.tile([P, W], U8, align_bytes=64)
            mxs[n] = (codes, scales)
            nc.vector.quantize_mx(
                out=codes[:].bitcast(FP8X4),
                scales=scales[:],
                in_=grps[n][:].rearrange("p w t -> p (w t)"),
            )

        def matmuls(n):
            codes, scales = mxs[n]
            for j in range(PACK):
                ps = psum.tile([P, W], F32, tag="bank")
                banks[(n, j)] = ps
                nc.tensor.matmul_mx(
                    out=ps[:],
                    lhsT=g_codes[:, j, :].bitcast(FP8X4),
                    lhsT_scale=g_scales[:, j, :],
                    rhs=codes[:].bitcast(FP8X4),
                    rhs_scale=scales[:],
                    start=True,
                    stop=True,
                )

        def rsqrts(n):
            r = r_pool.tile([P, PACK, W], F32)
            rs[n] = r
            for j in range(PACK):
                cuts = LAST_CUTS if (n, j) == (NB - 1, PACK - 1) else (0, W)
                for c0, c1 in zip(cuts[:-1], cuts[1:]):
                    nc.scalar.activation(
                        out=r[:, j, c0:c1], in_=banks[(n, j)][:, c0:c1],
                        func=ACT.Abs_reciprocal_sqrt, bias=beta[:, j : j + 1], scale=1.0,
                    )

        def out_chunk(n):
            b, l0 = n // (L // W), (n % (L // W)) * W
            return out[b].rearrange("(p j) l -> p j l", j=PACK)[:, :, l0 : l0 + W]

        xps = {}

        def x_to_psum(n):
            xs = x_chunk(n)
            pair = psum_x.tile([P, 2, W], BF16, tag="xp")
            single = psum_x.tile([P, 2, W], BF16, tag="xp")
            xps[n] = (pair, single)
            for j in range(3):
                nc.tensor.matmul(
                    xps[n][j // 2][:, j % 2, :], lhsT=ident_bf[:], rhs=xs[:, j, :],
                    start=True, stop=True,
                )

        def gpsimd_out(n):
            flat = grps[n + 2][:].rearrange("p w t -> p (w t)").bitcast(F32)
            return flat[:, 0:W]

        def gpsimd_product(n):
            nc.gpsimd.tensor_tensor(
                out=gpsimd_out(n), in0=rs[n][:, 3, :], in1=x_chunk(n)[:, 3, :], op=ALU.mult
            )

        def products_and_stores(n):
            xs = x_chunk(n)
            r = rs[n]
            out_v = out_chunk(n)
            if n in WINDOWS:
                pair, single = xps[n]
                nc.vector.tensor_tensor(
                    out=r[:, 0:2, :], in0=r[:, 0:2, :], in1=pair[:], op=ALU.mult
                )
                nc.sync.dma_start(out=out_v[:, 0:2, :], in_=r[:, 0:2, :])
                nc.vector.tensor_tensor(
                    out=r[:, 2, :], in0=r[:, 2, :], in1=single[:, 0, :], op=ALU.mult
                )
                nc.sync.dma_start(out=out_v[:, 2, :], in_=r[:, 2, :])
                nc.sync.dma_start(out=out_chunk(n - 1)[:, 3, :], in_=gpsimd_out(n - 1))
                groups = () if n + 1 in WINDOWS else ((3, 4),)
            elif n + 1 in WINDOWS:
                groups = ((0, 2), (2, 3))
            else:
                groups = tuple((j0, j0 + SG[n]) for j0 in range(0, PACK, SG[n]))
            for j0, j1 in groups:
                cuts = LAST_CUTS if (n, j0) == (NB - 1, PACK - 1) else (0, W)
                for c0, c1 in zip(cuts[:-1], cuts[1:]):
                    nc.vector.tensor_tensor(
                        out=r[:, j0:j1, c0:c1], in0=r[:, j0:j1, c0:c1], in1=xs[:, j0:j1, c0:c1],
                        op=ALU.mult,
                    )
                    nc.sync.dma_start(out=out_v[:, j0:j1, c0:c1], in_=r[:, j0:j1, c0:c1])

        gamma_floor(0)
        gamma_transposes(0)
        squares_act(0, 0, 144)
        gamma_floor(1)
        gamma_transposes(1)
        squares_dve(0, 144, 256)
        gamma_floor(2)
        gamma_transposes(2)
        gamma_floor(3)
        gamma_transposes(3)
        for j in range(PACK):
            gamma_square(j)
        gamma_round(0)
        squares_dve(0, 408, 512)
        gamma_round(1)
        gamma_quantise(0)
        gamma_round(2)
        gamma_quantise(1)
        beta_floor()
        gamma_round(3)
        gamma_quantise(2)
        beta_square()
        gamma_quantise(3)
        squares_act(0, 256, 408)
        quantise(0)
        beta_less_pedestal()
        matmuls(0)
        squares_act(1, 0, CA[1])
        squares_dve(1, CA[1], W)
        for n in range(NB):
            if n + 2 < NB:
                squares_dve(n + 2, CA[n + 2], W)
            if n + 1 < NB:
                quantise(n + 1)
            if n in WINDOWS:
                gpsimd_product(n - 1)
            rsqrts(n)
            if n + 1 in WINDOWS:
                x_to_psum(n + 1)
            if n + 1 < NB:
                matmuls(n + 1)
            if n + 2 < NB:
                squares_act(n + 2, 0, CA[n + 2])
            products_and_stores(n)
